import numpy as np
import ml_dtypes


def mxq(x, axis, fmt="e4m3"):
    dtype, down = {"e4m3": (ml_dtypes.float8_e4m3fn, 7), "e5m2": (ml_dtypes.float8_e5m2, 14)}[fmt]
    v = np.moveaxis(np.asarray(x, np.float32).astype(ml_dtypes.bfloat16).astype(np.float64), axis, -1)
    blocks = v.reshape(v.shape[:-1] + (-1, 32))
    amax = np.abs(blocks).max(-1, keepdims=True)
    byte = np.maximum(np.where(amax > 0, np.frexp(amax)[1] - 1 + 127, 0) - down, 1)
    scale = np.exp2(byte - 127.0)
    codes = (blocks / scale).astype(np.float32).astype(dtype).astype(np.float64)
    return np.moveaxis((codes * scale).reshape(v.shape), -1, axis)


WIDE = False


def mx_kscale(k):
    if not WIDE:
        return np.ones(k)
    levels = np.array([20, -20, 10, -10, 0])
    a = np.random.permutation(np.resize(levels, k // 512 * 4)).reshape(k // 512, 4)
    idx = np.arange(k)
    return np.exp2(a[idx // 512, idx % 128 // 32])


BF16 = ml_dtypes.bfloat16


def bf(x):
    return np.asarray(x, np.float32).astype(BF16)


def f64(x):
    return np.asarray(x).astype(np.float64)


B, C_IN, C_OUT, H, W = 2, 384, 512, 64, 64
P = 4
G = P * P
H4, W4 = H // P, W // P
T = B * H4 * W4


def to_groups(t):
    Bb, C, Hh, Ww = t.shape
    t = t.reshape(Bb, C, Hh // P, P, Ww // P, P).transpose(3, 5, 0, 2, 4, 1)
    return t.reshape(G, Bb * (Hh // P) * (Ww // P), C)


def setup_inputs():
    s = mx_kscale(T).reshape(B, H4, W4)
    s = np.repeat(np.repeat(s, P, axis=1), P, axis=2)[:, None, :, :]
    bound = np.sqrt(6.0 / (C_IN + C_OUT))
    x = np.random.standard_normal((B, C_IN, H, W)) * s
    Wg = np.random.uniform(-bound, bound, (G, C_OUT, C_IN))
    bg = np.random.standard_normal((G, C_OUT)) * 0.25
    g = np.random.standard_normal((B, C_OUT, H, W)) * np.exp2(np.random.randint(-12, 1, (B, 1, H, W))) / s
    return {"x": bf(x), "Wg": bf(Wg), "bg": bf(bg), "grad_out": bf(g)}


def reference(x, Wg, bg, grad_out):
    xg = mxq(to_groups(f64(x)), 1, "e4m3")
    gg = mxq(to_groups(f64(grad_out)), 1, "e5m2")
    return gg.transpose(0, 2, 1) @ xg

@@ -1,0 +1,207 @@
+from contextlib import ExitStack
+
+import concourse.mybir as mybir
+from concourse.masks import make_identity
+
+BF16 = mybir.dt.bfloat16
+F32 = mybir.dt.float32
+U32 = mybir.dt.uint32
+U8 = mybir.dt.uint8
+E4X4 = mybir.dt.float8_e4m3fn_x4
+E5X4 = mybir.dt.float8_e5m2_x4
+
+P = 128
+C_IN = 384
+C_OUT = 512
+GROUPS = 16
+PIX = 4096
+BLK = 64
+NBX = C_IN // BLK
+NBG = C_OUT // BLK
+
+FLOPS = 2 * GROUPS * 512 * C_OUT * C_IN
+BYTES = 2 * 2 * C_IN * PIX + 2 * 2 * C_OUT * PIX + 4 * GROUPS * C_OUT * C_IN
+
+
+def tile_groupwiselinearprojector_kernel(tc, x, Wg, bg, grad_out, out):
+    nc = tc.nc
+    with ExitStack() as ctx:
+        const = ctx.enter_context(tc.tile_pool(name="const", bufs=1))
+        rawp = ctx.enter_context(tc.tile_pool(name="rawp", bufs=6))
+        srtp = ctx.enter_context(tc.tile_pool(name="srtp", bufs=4))
+        grpp = ctx.enter_context(tc.tile_pool(name="grpp", bufs=6))
+        keep = ctx.enter_context(tc.tile_pool(name="keep", bufs=1))
+        ostp = ctx.enter_context(tc.tile_pool(name="ostp", bufs=3))
+        tpp = ctx.enter_context(tc.psum_pool(name="tpp", bufs=4))
+        accp = ctx.enter_context(tc.psum_pool(name="accp", bufs=4))
+        ctx.enter_context(tc.manual_schedule())
+
+        ident = const.tile([P, P], BF16, name="ident")
+        make_identity(nc, ident[:])
+        perm = const.tile([P, P], BF16, name="perm")
+        nc.vector.tensor_copy(
+            out=perm[:].rearrange("p (i c b) -> p i c b", i=2, b=2),
+            in_=ident[:].rearrange("p (c i b) -> p i c b", i=2, b=2),
+        )
+
+        xc = keep.tile([P, GROUPS * C_IN], U32, name="xc", align_bytes=64)
+        xs = keep.tile([P, GROUPS * C_IN], U8, name="xs", align_bytes=64)
+        gcs = []
+        gss = []
+        for c2 in range(2):
+            gcs.append(keep.tile([P, GROUPS * 256], U32, name="gc%d" % c2, align_bytes=64))
+            gss.append(keep.tile([P, GROUPS * 256], U8, name="gs%d" % c2, align_bytes=64))
+
+        blocks = [(x, k) for k in range(NBX)] + [(grad_out, k) for k in range(NBG)]
+        raws = []
+        for src, k in blocks:
+            raw = rawp.tile([P, PIX], BF16, name="raw")
+            for b in range(2):
+                nc.sync.dma_start(
+                    out=raw[b:P:2, :],
+                    in_=src[b, k * BLK : (k + 1) * BLK].rearrange("c h w -> c (h w)"),
+                )
+            raws.append(raw)
+
+        srts = {}
+        grps = {}
+        state = {"copies": 0, "pattern": "VS"}
+
+        def sort_block(s, pieces):
+            srt = srtp.tile([P, PIX], BF16, name="srt")
+            dst = srt[:].bitcast(F32).rearrange("p (a h r c) -> p a h r c", a=4, h=2, r=16)
+            src = raws[s][:].bitcast(F32).rearrange("p (r a c h) -> p a h r c", a=4, h=2, r=16)
+            step = 4 // pieces
+            for a in range(0, 4, step):
+                nc.vector.tensor_copy(out=dst[:, a : a + step], in_=src[:, a : a + step])
+            srts[s] = srt
+
+        def grouped(key):
+            if key not in grps:
+                grps[key] = grpp.tile([P, 4096], BF16, name="grp", align_bytes=64)
+            return grps[key]
+
+        def banks(s, pr):
+            is_g = s >= NBX
+            words = srts[s][:].rearrange("p (w e) -> p w e", e=2)
+            for h in range(2):
+                tp = tpp.tile([P, 512], BF16, name="tp")
+                for e in range(2):
+                    for rh in range(2):
+                        w0 = (pr * 2 + h) * 256 + rh * 128
+                        src = words[:, w0 : w0 + 128, e]
+                        if is_g:
+                            dst = tp[:].rearrange("p (e i r n) -> p e i r n", e=2, i=2, r=2)[:, e, :, rh, :]
+                            nc.tensor.transpose(dst, src, perm[:])
+                        else:
+                            dst = tp[:, (e * 2 + rh) * 128 : (e * 2 + rh + 1) * 128]
+                            nc.tensor.transpose(dst, src, ident[:])
+                if is_g:
+                    kb = (s - NBX) % 4
+                    grp = grouped(("g", (s - NBX) // 4, pr))
+                    nc.scalar.copy(
+                        out=grp[:]
+                        .bitcast(F32)
+                        .rearrange("p (a m r) -> p a m r", a=8, r=2)[:, h * 4 : h * 4 + 4, kb * 32 : (kb + 1) * 32, :],
+                        in_=tp[:].bitcast(F32).rearrange("p (a r c) -> p a c r", a=4, r=2),
+                    )
+                else:
+                    kb = s % 2
+                    gl = (pr % 2) * 4 + 2 * h
+                    grp = grouped(("x", s // 2, pr // 2))
+                    nc.scalar.copy(
+                        out=grp[:]
+                        .bitcast(F32)
+                        .rearrange("p (g c r) -> p g c r", g=8, r=2)[:, gl : gl + 2, kb * 64 : (kb + 1) * 64, :],
+                        in_=tp[:].bitcast(F32).rearrange("p (e r c) -> p e c r", e=2, r=2),
+                    )
+
+        def quant_x(chunk, half):
+            grp = grps[("x", chunk, half)]
+            for gl in range(8):
+                col = (half * 8 + gl) * C_IN + chunk * 128
+                nc.vector.quantize_mx(
+                    out=xc[:, col : col + 128].bitcast(E4X4),
+                    scales=xs[:, col : col + 128],
+                    in_=grp[:, gl * 512 : (gl + 1) * 512],
+                )
+
+        def quant_g(c2, pr):
+            nc.vector.quantize_mx(
+                out=gcs[c2][:, pr * 1024 : (pr + 1) * 1024].bitcast(E5X4),
+                scales=gss[c2][:, pr * 1024 : (pr + 1) * 1024],
+                in_=grps[("g", c2, pr)][:],
+            )
+
+        def passes(c2, pr, pattern):
+            state["pattern"] = pattern
+            for g0 in range(pr * 4, pr * 4 + 4, 2):
+                ost = ostp.tile([P, 2, 2, C_IN], F32, name="ost")
+                for gl in range(2):
+                    grp = g0 + gl
+                    lo = grp * C_IN
+                    skip = 0
+                    if lo + 512 > GROUPS * C_IN:
+                        skip = lo + 512 - GROUPS * C_IN
+                        lo = lo - skip
+                    for i in range(2):
+                        acc = accp.tile([P, 512], F32, name="acc")
+                        w0 = (grp * 2 + i) * 128
+                        nc.tensor.matmul_mx(
+                            out=acc[:],
+                            lhsT=gcs[c2][:, w0 : w0 + 128].bitcast(E5X4),
+                            lhsT_scale=gss[c2][:, w0 : w0 + 128],
+                            rhs=xc[:, lo : lo + 512].bitcast(E4X4),
+                            rhs_scale=xs[:, lo : lo + 512],
+                            start=True,
+                            stop=True,
+                        )
+                        pat = state["pattern"]
+                        if pat[state["copies"] % len(pat)] == "V":
+                            nc.vector.tensor_copy(out=ost[:, gl, i, :], in_=acc[:, skip : skip + C_IN])
+                        else:
+                            nc.scalar.copy(out=ost[:, gl, i, :], in_=acc[:, skip : skip + C_IN])
+                        state["copies"] += 1
+                nc.sync.dma_start(
+                    out=out[g0 : g0 + 2, c2 * 256 : (c2 + 1) * 256, :].rearrange("g (m i) c -> m g (i c)", i=2),
+                    in_=ost[:].rearrange("p g i c -> p g (i c)"),
+                )
+
+        def burst(k):
+            for s in ((10, 11) if k < 4 else (12, 13)):
+                banks(s, k % 4)
+
+        sort_block(0, 4)
+        sort_block(1, 1)
+        for n in range(10):
+            sort_block(n + 2, 1)
+            for pr in range(4):
+                banks(n, pr)
+            if 2 <= n < 8:
+                quant_x((n - 2) // 2, n % 2)
+        quant_g(0, 0)
+        sort_block(12, 1)
+        burst(0)
+        quant_g(0, 1)
+        burst(1)
+        passes(0, 0, "SSVS")
+        sort_block(13, 1)
+        quant_g(0, 2)
+        burst(2)
+        passes(0, 1, "SSVS")
+        quant_g(0, 3)
+        burst(3)
+        passes(0, 2, "VS")
+        burst(4)
+        passes(0, 3, "VS")
+        quant_g(1, 0)
+        burst(5)
+        passes(1, 0, "VS")
+        quant_g(1, 1)
+        burst(6)
+        passes(1, 1, "VS")
+        quant_g(1, 2)
+        burst(7)
+        quant_g(1, 3)
+        passes(1, 2, "SSVS")
+        passes(1, 3, "VS")

@@ -31,9 +31,8 @@ def tile_groupwiselinearprojector_kernel(tc, x, Wg, bg, grad_out, out):
         srtp = ctx.enter_context(tc.tile_pool(name="srtp", bufs=4))
         grpp = ctx.enter_context(tc.tile_pool(name="grpp", bufs=6))
         keep = ctx.enter_context(tc.tile_pool(name="keep", bufs=1))
-        ostp = ctx.enter_context(tc.tile_pool(name="ostp", bufs=3))
-        tpp = ctx.enter_context(tc.psum_pool(name="tpp", bufs=4))
-        accp = ctx.enter_context(tc.psum_pool(name="accp", bufs=4))
+        ostp = ctx.enter_context(tc.tile_pool(name="ostp", bufs=5))
+        psp = ctx.enter_context(tc.psum_pool(name="psp", bufs=8))
         ctx.enter_context(tc.manual_schedule())
 
         ident = const.tile([P, P], BF16, name="ident")
@@ -85,7 +84,7 @@ def tile_groupwiselinearprojector_kernel(tc, x, Wg, bg, grad_out, out):
             is_g = s >= NBX
             words = srts[s][:].rearrange("p (w e) -> p w e", e=2)
             for h in range(2):
-                tp = tpp.tile([P, 512], BF16, name="tp")
+                tp = psp.tile([P, 512], BF16, name="tp", tag="bank")
                 for e in range(2):
                     for rh in range(2):
                         w0 = (pr * 2 + h) * 256 + rh * 128
@@ -145,7 +144,7 @@ def tile_groupwiselinearprojector_kernel(tc, x, Wg, bg, grad_out, out):
                         skip = lo + 512 - GROUPS * C_IN
                         lo = lo - skip
                     for i in range(2):
-                        acc = accp.tile([P, 512], F32, name="acc")
+                        acc = psp.tile([P, 512], F32, name="acc", tag="bank")
                         w0 = (grp * 2 + i) * 128
                         nc.tensor.matmul_mx(
                             out=acc[:],

@@ -42,6 +42,13 @@ def tile_groupwiselinearprojector_kernel(tc, x, Wg, bg, grad_out, out):
             out=perm[:].rearrange("p (i c b) -> p i c b", i=2, b=2),
             in_=ident[:].rearrange("p (c i b) -> p i c b", i=2, b=2),
         )
+        wide = const.tile([P, 512], BF16, name="wide")
+        nc.vector.memset(wide[:], 1.0)
+        dum = psp.tile([P, 512], F32, name="dum", tag="bank")
+
+        def dummy(n):
+            for k in range(n):
+                nc.tensor.matmul(dum[:], lhsT=ident[:], rhs=wide[:], start=True, stop=True)
 
         xc = keep.tile([P, GROUPS * C_IN], U32, name="xc", align_bytes=64)
         xs = keep.tile([P, GROUPS * C_IN], U8, name="xs", align_bytes=64)
@@ -61,6 +68,7 @@ def tile_groupwiselinearprojector_kernel(tc, x, Wg, bg, grad_out, out):
                     in_=src[b, k * BLK : (k + 1) * BLK].rearrange("c h w -> c (h w)"),
                 )
             raws.append(raw)
+        dummy(10)
 
         srts = {}
         grps = {}

@@ -42,13 +42,6 @@ def tile_groupwiselinearprojector_kernel(tc, x, Wg, bg, grad_out, out):
             out=perm[:].rearrange("p (i c b) -> p i c b", i=2, b=2),
             in_=ident[:].rearrange("p (c i b) -> p i c b", i=2, b=2),
         )
-        wide = const.tile([P, 512], BF16, name="wide")
-        nc.vector.memset(wide[:], 1.0)
-        dum = psp.tile([P, 512], F32, name="dum", tag="bank")
-
-        def dummy(n):
-            for k in range(n):
-                nc.tensor.matmul(dum[:], lhsT=ident[:], rhs=wide[:], start=True, stop=True)
 
         xc = keep.tile([P, GROUPS * C_IN], U32, name="xc", align_bytes=64)
         xs = keep.tile([P, GROUPS * C_IN], U8, name="xs", align_bytes=64)
@@ -68,11 +61,9 @@ def tile_groupwiselinearprojector_kernel(tc, x, Wg, bg, grad_out, out):
                     in_=src[b, k * BLK : (k + 1) * BLK].rearrange("c h w -> c (h w)"),
                 )
             raws.append(raw)
-        dummy(10)
 
         srts = {}
         grps = {}
-        state = {"copies": 0, "pattern": "VS"}
 
         def sort_block(s, pieces):
             srt = srtp.tile([P, PIX], BF16, name="srt")
@@ -140,75 +131,114 @@ def tile_groupwiselinearprojector_kernel(tc, x, Wg, bg, grad_out, out):
                 in_=grps[("g", c2, pr)][:],
             )
 
-        def passes(c2, pr, pattern):
-            state["pattern"] = pattern
-            for g0 in range(pr * 4, pr * 4 + 4, 2):
-                ost = ostp.tile([P, 2, 2, C_IN], F32, name="ost")
-                for gl in range(2):
-                    grp = g0 + gl
-                    lo = grp * C_IN
-                    skip = 0
-                    if lo + 512 > GROUPS * C_IN:
-                        skip = lo + 512 - GROUPS * C_IN
-                        lo = lo - skip
-                    for i in range(2):
-                        acc = psp.tile([P, 512], F32, name="acc", tag="bank")
-                        w0 = (grp * 2 + i) * 128
-                        nc.tensor.matmul_mx(
-                            out=acc[:],
-                            lhsT=gcs[c2][:, w0 : w0 + 128].bitcast(E5X4),
-                            lhsT_scale=gss[c2][:, w0 : w0 + 128],
-                            rhs=xc[:, lo : lo + 512].bitcast(E4X4),
-                            rhs_scale=xs[:, lo : lo + 512],
-                            start=True,
-                            stop=True,
-                        )
-                        pat = state["pattern"]
-                        if pat[state["copies"] % len(pat)] == "V":
-                            nc.vector.tensor_copy(out=ost[:, gl, i, :], in_=acc[:, skip : skip + C_IN])
-                        else:
-                            nc.scalar.copy(out=ost[:, gl, i, :], in_=acc[:, skip : skip + C_IN])
-                        state["copies"] += 1
-                nc.sync.dma_start(
-                    out=out[g0 : g0 + 2, c2 * 256 : (c2 + 1) * 256, :].rearrange("g (m i) c -> m g (i c)", i=2),
-                    in_=ost[:].rearrange("p g i c -> p g (i c)"),
-                )
-
-        def burst(k):
-            for s in ((10, 11) if k < 4 else (12, 13)):
-                banks(s, k % 4)
+        def passes(c2, pr, gp, pattern):
+            g0 = pr * 4 + gp * 2
+            ost = ostp.tile([P, 2, 2, C_IN], F32, name="ost")
+            for gl in range(2):
+                grp = g0 + gl
+                lo = grp * C_IN
+                skip = 0
+                if lo + 512 > GROUPS * C_IN:
+                    skip = lo + 512 - GROUPS * C_IN
+                    lo = lo - skip
+                for i in range(2):
+                    acc = psp.tile([P, 512], F32, name="acc", tag="bank")
+                    w0 = (grp * 2 + i) * 128
+                    nc.tensor.matmul_mx(
+                        out=acc[:],
+                        lhsT=gcs[c2][:, w0 : w0 + 128].bitcast(E5X4),
+                        lhsT_scale=gss[c2][:, w0 : w0 + 128],
+                        rhs=xc[:, lo : lo + 512].bitcast(E4X4),
+                        rhs_scale=xs[:, lo : lo + 512],
+                        start=True,
+                        stop=True,
+                    )
+                    if pattern[gl * 2 + i] == "V":
+                        nc.vector.tensor_copy(out=ost[:, gl, i, :], in_=acc[:, skip : skip + C_IN])
+                    else:
+                        nc.scalar.copy(out=ost[:, gl, i, :], in_=acc[:, skip : skip + C_IN])
+            nc.sync.dma_start(
+                out=out[g0 : g0 + 2, c2 * 256 : (c2 + 1) * 256, :].rearrange("g (m i) c -> m g (i c)", i=2),
+                in_=ost[:].rearrange("p g i c -> p g (i c)"),
+            )
 
         sort_block(0, 4)
         sort_block(1, 1)
-        for n in range(10):
-            sort_block(n + 2, 1)
-            for pr in range(4):
-                banks(n, pr)
-            if 2 <= n < 8:
-                quant_x((n - 2) // 2, n % 2)
+        sort_block(2, 1)
+        for pr in range(4):
+            banks(0, pr)
+        sort_block(3, 1)
+        for pr in range(4):
+            banks(1, pr)
+        sort_block(4, 1)
+        for pr in range(4):
+            banks(2, pr)
+        quant_x(0, 0)
+        sort_block(5, 1)
+        for pr in range(4):
+            banks(3, pr)
+        quant_x(0, 1)
+        sort_block(6, 1)
+        for pr in range(4):
+            banks(4, pr)
+        quant_x(1, 0)
+        sort_block(7, 1)
+        for pr in range(4):
+            banks(5, pr)
+        quant_x(1, 1)
+        sort_block(8, 1)
+        quant_x(2, 0)
+        for pr in range(4):
+            banks(6, pr)
+        for pr in range(4):
+            banks(7, pr)
+        sort_block(9, 1)
+        quant_x(2, 1)
+        sort_block(10, 1)
+        sort_block(11, 1)
+        for pr in range(4):
+            banks(8, pr)
+        for pr in range(4):
+            banks(9, pr)
         quant_g(0, 0)
-        sort_block(12, 1)
-        burst(0)
-        quant_g(0, 1)
-        burst(1)
-        passes(0, 0, "SSVS")
-        sort_block(13, 1)
+        banks(10, 1)
+        banks(10, 0)
+        banks(11, 3)
+        banks(11, 0)
         quant_g(0, 2)
-        burst(2)
-        passes(0, 1, "SSVS")
+        passes(0, 0, 1, "VVSS")
+        quant_g(0, 1)
+        passes(0, 0, 0, "SVSS")
+        passes(0, 2, 1, "VSSS")
+        sort_block(12, 1)
+        passes(0, 1, 1, "VSSV")
+        passes(0, 1, 0, "VSSV")
+        banks(12, 1)
+        sort_block(13, 1)
+        banks(12, 0)
         quant_g(0, 3)
-        burst(3)
-        passes(0, 2, "VS")
-        burst(4)
-        passes(0, 3, "VS")
+        banks(12, 2)
+        passes(0, 2, 0, "VSSV")
+        banks(13, 0)
         quant_g(1, 0)
-        burst(5)
-        passes(1, 0, "VS")
+        banks(11, 1)
+        banks(13, 1)
+        passes(0, 3, 0, "SVVS")
+        passes(0, 3, 1, "VSSV")
+        passes(1, 0, 0, "VSSV")
+        banks(13, 2)
         quant_g(1, 1)
-        burst(6)
-        passes(1, 1, "VS")
+        banks(11, 2)
+        banks(10, 2)
+        passes(1, 0, 1, "SVVS")
+        passes(1, 1, 1, "VSSS")
         quant_g(1, 2)
-        burst(7)
+        passes(1, 1, 0, "VVSS")
+        banks(13, 3)
+        banks(12, 3)
+        banks(10, 3)
+        passes(1, 2, 1, "VSVS")
         quant_g(1, 3)
-        passes(1, 2, "SSVS")
-        passes(1, 3, "VS")
+        passes(1, 2, 0, "SSVS")
+        passes(1, 3, 0, "SVVS")
+        passes(1, 3, 1, "SSVS")

@@ -186,59 +186,67 @@ def tile_groupwiselinearprojector_kernel(tc, x, Wg, bg, grad_out, out):
         for pr in range(4):
             banks(5, pr)
         quant_x(1, 1)
+        banks(6, 0)
+        banks(6, 2)
         sort_block(8, 1)
-        quant_x(2, 0)
-        for pr in range(4):
-            banks(6, pr)
-        for pr in range(4):
-            banks(7, pr)
-        sort_block(9, 1)
         quant_x(2, 1)
+        banks(6, 3)
+        banks(6, 1)
+        sort_block(9, 1)
+        banks(7, 0)
+        banks(7, 3)
+        banks(7, 2)
+        banks(7, 1)
+        quant_x(2, 0)
+        banks(8, 0)
+        banks(8, 2)
+        banks(8, 3)
+        banks(9, 0)
+        banks(9, 1)
+        banks(9, 2)
         sort_block(10, 1)
-        sort_block(11, 1)
-        for pr in range(4):
-            banks(8, pr)
-        for pr in range(4):
-            banks(9, pr)
+        banks(9, 3)
+        banks(8, 1)
         quant_g(0, 0)
-        banks(10, 1)
-        banks(10, 0)
-        banks(11, 3)
-        banks(11, 0)
         quant_g(0, 2)
-        passes(0, 0, 1, "VVSS")
+        banks(10, 1)
         quant_g(0, 1)
-        passes(0, 0, 0, "SVSS")
+        passes(0, 0, 0, "SSVS")
+        passes(0, 2, 0, "SVSS")
+        sort_block(11, 1)
+        banks(10, 0)
+        passes(0, 1, 0, "VSVS")
         passes(0, 2, 1, "VSSS")
         sort_block(12, 1)
-        passes(0, 1, 1, "VSSV")
-        passes(0, 1, 0, "VSSV")
-        banks(12, 1)
+        passes(0, 1, 1, "SVSV")
+        passes(0, 0, 1, "SVVS")
+        banks(10, 2)
         sort_block(13, 1)
+        banks(11, 0)
+        banks(11, 2)
+        banks(11, 1)
         banks(12, 0)
         quant_g(0, 3)
-        banks(12, 2)
-        passes(0, 2, 0, "VSSV")
+        banks(12, 1)
         banks(13, 0)
+        passes(0, 3, 1, "VSVS")
         quant_g(1, 0)
-        banks(11, 1)
+        passes(0, 3, 0, "SVSV")
         banks(13, 1)
-        passes(0, 3, 0, "SVVS")
-        passes(0, 3, 1, "VSSV")
-        passes(1, 0, 0, "VSSV")
-        banks(13, 2)
         quant_g(1, 1)
-        banks(11, 2)
-        banks(10, 2)
+        banks(12, 2)
+        passes(1, 0, 0, "SSVS")
         passes(1, 0, 1, "SVVS")
-        passes(1, 1, 1, "VSSS")
-        quant_g(1, 2)
-        passes(1, 1, 0, "VVSS")
-        banks(13, 3)
-        banks(12, 3)
+        passes(1, 1, 0, "VSSV")
+        passes(1, 1, 1, "SVSV")
+        banks(13, 2)
+        banks(11, 3)
         banks(10, 3)
-        passes(1, 2, 1, "VSVS")
+        banks(12, 3)
+        banks(13, 3)
+        quant_g(1, 2)
+        passes(1, 2, 1, "SVVS")
         quant_g(1, 3)
-        passes(1, 2, 0, "SSVS")
-        passes(1, 3, 0, "SVVS")
-        passes(1, 3, 1, "SSVS")
+        passes(1, 2, 0, "VSSS")
+        passes(1, 3, 1, "VSVS")
+        passes(1, 3, 0, "SSVS")

@@ -55,11 +55,10 @@ def tile_groupwiselinearprojector_kernel(tc, x, Wg, bg, grad_out, out):
         raws = []
         for src, k in blocks:
             raw = rawp.tile([P, PIX], BF16, name="raw")
-            for b in range(2):
-                nc.sync.dma_start(
-                    out=raw[b:P:2, :],
-                    in_=src[b, k * BLK : (k + 1) * BLK].rearrange("c h w -> c (h w)"),
-                )
+            nc.sync.dma_start(
+                out=raw[:].rearrange("p (b f) -> p b f", b=2),
+                in_=src[:, k * BLK : (k + 1) * BLK].rearrange("b c (u h) w -> (c u) b (h w)", u=2),
+            )
             raws.append(raw)
 
         srts = {}

@@ -113,15 +113,15 @@ def tile_groupwiselinearprojector_kernel(tc, x, Wg, bg, grad_out, out):
                         in_=tp[:].bitcast(F32).rearrange("p (e r c) -> p e c r", e=2, r=2),
                     )
 
-        def quant_x(chunk, half):
-            grp = grps[("x", chunk, half)]
-            for gl in range(8):
-                col = (half * 8 + gl) * C_IN + chunk * 128
-                nc.vector.quantize_mx(
-                    out=xc[:, col : col + 128].bitcast(E4X4),
-                    scales=xs[:, col : col + 128],
-                    in_=grp[:, gl * 512 : (gl + 1) * 512],
-                )
+        def quant_x(chunk, grp_no):
+            grp = grps[("x", chunk, grp_no // 8)]
+            gl = grp_no % 8
+            col = grp_no * C_IN + chunk * 128
+            nc.vector.quantize_mx(
+                out=xc[:, col : col + 128].bitcast(E4X4),
+                scales=xs[:, col : col + 128],
+                in_=grp[:, gl * 512 : (gl + 1) * 512],
+            )
 
         def quant_g(c2, pr):
             nc.vector.quantize_mx(
@@ -161,51 +161,21 @@ def tile_groupwiselinearprojector_kernel(tc, x, Wg, bg, grad_out, out):
                 in_=ost[:].rearrange("p g i c -> p g (i c)"),
             )
 
+        x_calls = [(chunk, grp_no) for chunk in range(3) for grp_no in range(GROUPS)]
+        issued = 0
         sort_block(0, 4)
-        sort_block(1, 1)
-        sort_block(2, 1)
-        for pr in range(4):
-            banks(0, pr)
-        sort_block(3, 1)
-        for pr in range(4):
-            banks(1, pr)
-        sort_block(4, 1)
-        for pr in range(4):
-            banks(2, pr)
-        quant_x(0, 0)
-        sort_block(5, 1)
-        for pr in range(4):
-            banks(3, pr)
-        quant_x(0, 1)
-        sort_block(6, 1)
-        for pr in range(4):
-            banks(4, pr)
-        quant_x(1, 0)
-        sort_block(7, 1)
-        for pr in range(4):
-            banks(5, pr)
-        quant_x(1, 1)
-        banks(6, 0)
-        banks(6, 2)
-        sort_block(8, 1)
-        quant_x(2, 1)
-        banks(6, 3)
-        banks(6, 1)
-        sort_block(9, 1)
-        banks(7, 0)
-        banks(7, 3)
-        banks(7, 2)
-        banks(7, 1)
-        quant_x(2, 0)
-        banks(8, 0)
-        banks(8, 2)
-        banks(8, 3)
-        banks(9, 0)
-        banks(9, 1)
-        banks(9, 2)
+        for s in range(10):
+            if s < 9:
+                sort_block(s + 1, 1)
+            for pr in range(4):
+                banks(s, pr)
+            ready = GROUPS * ((min(s, NBX - 1) + 1) // 2)
+            upto = min(ready, issued + 7)
+            for chunk, grp_no in x_calls[issued:upto]:
+                quant_x(chunk, grp_no)
+            issued = upto
+        assert issued == len(x_calls)
         sort_block(10, 1)
-        banks(9, 3)
-        banks(8, 1)
         quant_g(0, 0)
         quant_g(0, 2)
         banks(10, 1)

@@ -124,11 +124,13 @@ def tile_groupwiselinearprojector_kernel(tc, x, Wg, bg, grad_out, out):
             )
 
         def quant_g(c2, pr):
-            nc.vector.quantize_mx(
-                out=gcs[c2][:, pr * 1024 : (pr + 1) * 1024].bitcast(E5X4),
-                scales=gss[c2][:, pr * 1024 : (pr + 1) * 1024],
-                in_=grps[("g", c2, pr)][:],
-            )
+            for gp in range(2):
+                w0 = pr * 1024 + gp * 512
+                nc.vector.quantize_mx(
+                    out=gcs[c2][:, w0 : w0 + 512].bitcast(E5X4),
+                    scales=gss[c2][:, w0 : w0 + 512],
+                    in_=grps[("g", c2, pr)][:, gp * 2048 : (gp + 1) * 2048],
+                )
 
         def passes(c2, pr, gp, pattern):
             g0 = pr * 4 + gp * 2

@@ -78,10 +78,10 @@ def tile_groupwiselinearprojector_kernel(tc, x, Wg, bg, grad_out, out):
                 grps[key] = grpp.tile([P, 4096], BF16, name="grp", align_bytes=64)
             return grps[key]
 
-        def banks(s, pr):
+        def banks(s, pr, halves=(0, 1)):
             is_g = s >= NBX
             words = srts[s][:].rearrange("p (w e) -> p w e", e=2)
-            for h in range(2):
+            for h in halves:
                 tp = psp.tile([P, 512], BF16, name="tp", tag="bank")
                 for e in range(2):
                     for rh in range(2):
@@ -123,8 +123,8 @@ def tile_groupwiselinearprojector_kernel(tc, x, Wg, bg, grad_out, out):
                 in_=grp[:, gl * 512 : (gl + 1) * 512],
             )
 
-        def quant_g(c2, pr):
-            for gp in range(2):
+        def quant_g(c2, pr, pairs=(0, 1)):
+            for gp in pairs:
                 w0 = pr * 1024 + gp * 512
                 nc.vector.quantize_mx(
                     out=gcs[c2][:, w0 : w0 + 512].bitcast(E5X4),
@@ -132,9 +132,10 @@ def tile_groupwiselinearprojector_kernel(tc, x, Wg, bg, grad_out, out):
                     in_=grps[("g", c2, pr)][:, gp * 2048 : (gp + 1) * 2048],
                 )
 
-        def passes(c2, pr, gp, pattern):
+        def passes(c2, pr, gp, pattern, fine=False):
             g0 = pr * 4 + gp * 2
             ost = ostp.tile([P, 2, 2, C_IN], F32, name="ost")
+            rows = slice(c2 * 256, (c2 + 1) * 256)
             for gl in range(2):
                 grp = g0 + gl
                 lo = grp * C_IN
@@ -158,10 +159,21 @@ def tile_groupwiselinearprojector_kernel(tc, x, Wg, bg, grad_out, out):
                         nc.vector.tensor_copy(out=ost[:, gl, i, :], in_=acc[:, skip : skip + C_IN])
                     else:
                         nc.scalar.copy(out=ost[:, gl, i, :], in_=acc[:, skip : skip + C_IN])
-            nc.sync.dma_start(
-                out=out[g0 : g0 + 2, c2 * 256 : (c2 + 1) * 256, :].rearrange("g (m i) c -> m g (i c)", i=2),
-                in_=ost[:].rearrange("p g i c -> p g (i c)"),
-            )
+                    if fine and gl == 1:
+                        nc.sync.dma_start(
+                            out=out[grp, rows, :].rearrange("(m i) c -> i m c", i=2)[i],
+                            in_=ost[:, gl, i, :],
+                        )
+                if fine and gl == 0:
+                    nc.sync.dma_start(
+                        out=out[grp, rows, :].rearrange("(m i) c -> m (i c)", i=2),
+                        in_=ost[:, gl].rearrange("p i c -> p (i c)"),
+                    )
+            if not fine:
+                nc.sync.dma_start(
+                    out=out[g0 : g0 + 2, rows, :].rearrange("g (m i) c -> m g (i c)", i=2),
+                    in_=ost[:].rearrange("p g i c -> p g (i c)"),
+                )
 
         x_calls = [(chunk, grp_no) for chunk in range(3) for grp_no in range(GROUPS)]
         issued = 0
@@ -179,45 +191,44 @@ def tile_groupwiselinearprojector_kernel(tc, x, Wg, bg, grad_out, out):
         assert issued == len(x_calls)
         sort_block(10, 1)
         quant_g(0, 0)
-        quant_g(0, 2)
-        banks(10, 1)
         quant_g(0, 1)
-        passes(0, 0, 0, "SSVS")
-        passes(0, 2, 0, "SVSS")
-        sort_block(11, 1)
         banks(10, 0)
-        passes(0, 1, 0, "VSVS")
-        passes(0, 2, 1, "VSSS")
-        sort_block(12, 1)
+        quant_g(0, 2)
+        passes(0, 0, 0, "SSVS")
+        passes(0, 0, 1, "SVSV")
+        sort_block(11, 1)
+        banks(10, 1)
+        passes(0, 1, 0, "SSVS")
         passes(0, 1, 1, "SVSV")
-        passes(0, 0, 1, "SVVS")
+        sort_block(12, 1)
+        passes(0, 2, 0, "SSVS")
+        passes(0, 2, 1, "SVSV")
         banks(10, 2)
         sort_block(13, 1)
         banks(11, 0)
-        banks(11, 2)
         banks(11, 1)
+        banks(11, 2)
         banks(12, 0)
         quant_g(0, 3)
         banks(12, 1)
         banks(13, 0)
-        passes(0, 3, 1, "VSVS")
-        quant_g(1, 0)
         passes(0, 3, 0, "SVSV")
+        quant_g(1, 0)
+        passes(0, 3, 1, "SSVS")
         banks(13, 1)
         quant_g(1, 1)
         banks(12, 2)
-        passes(1, 0, 0, "SSVS")
-        passes(1, 0, 1, "SVVS")
-        passes(1, 1, 0, "VSSV")
-        passes(1, 1, 1, "SVSV")
         banks(13, 2)
-        banks(11, 3)
-        banks(10, 3)
-        banks(12, 3)
-        banks(13, 3)
+        passes(1, 0, 0, "SVSV")
         quant_g(1, 2)
-        passes(1, 2, 1, "SVVS")
-        quant_g(1, 3)
-        passes(1, 2, 0, "VSSS")
-        passes(1, 3, 1, "VSVS")
+        passes(1, 0, 1, "SSVS")
+        passes(1, 1, 0, "SVSV")
+        passes(1, 1, 1, "SVSV")
+        passes(1, 2, 0, "SVSV")
+        passes(1, 2, 1, "SVSV")
+        for h in range(2):
+            for s in range(10, 14):
+                banks(s, 3, (h,))
+            quant_g(1, 3, (h,))
         passes(1, 3, 0, "SSVS")
+        passes(1, 3, 1, "SVSV", fine=True)

@@ -27,9 +27,9 @@ def tile_groupwiselinearprojector_kernel(tc, x, Wg, bg, grad_out, out):
     nc = tc.nc
     with ExitStack() as ctx:
         const = ctx.enter_context(tc.tile_pool(name="const", bufs=1))
-        rawp = ctx.enter_context(tc.tile_pool(name="rawp", bufs=6))
+        rawp = ctx.enter_context(tc.tile_pool(name="rawp", bufs=5))
         srtp = ctx.enter_context(tc.tile_pool(name="srtp", bufs=4))
-        grpp = ctx.enter_context(tc.tile_pool(name="grpp", bufs=6))
+        grpp = ctx.enter_context(tc.tile_pool(name="grpp", bufs=7))
         keep = ctx.enter_context(tc.tile_pool(name="keep", bufs=1))
         ostp = ctx.enter_context(tc.tile_pool(name="ostp", bufs=5))
         psp = ctx.enter_context(tc.psum_pool(name="psp", bufs=8))
@@ -184,7 +184,7 @@ def tile_groupwiselinearprojector_kernel(tc, x, Wg, bg, grad_out, out):
             for pr in range(4):
                 banks(s, pr)
             ready = GROUPS * ((min(s, NBX - 1) + 1) // 2)
-            upto = min(ready, issued + 7)
+            upto = min(ready, issued + 6)
             for chunk, grp_no in x_calls[issued:upto]:
                 quant_x(chunk, grp_no)
             issued = upto

from contextlib import ExitStack

import concourse.mybir as mybir
from concourse.masks import make_identity

BF16 = mybir.dt.bfloat16
F32 = mybir.dt.float32
U32 = mybir.dt.uint32
U8 = mybir.dt.uint8
E4X4 = mybir.dt.float8_e4m3fn_x4
E5X4 = mybir.dt.float8_e5m2_x4

P = 128
C_IN = 384
C_OUT = 512
GROUPS = 16
PIX = 4096
BLK = 64
NBX = C_IN // BLK
NBG = C_OUT // BLK

FLOPS = 2 * GROUPS * 512 * C_OUT * C_IN
BYTES = 2 * 2 * C_IN * PIX + 2 * 2 * C_OUT * PIX + 4 * GROUPS * C_OUT * C_IN


def tile_groupwiselinearprojector_kernel(tc, x, Wg, bg, grad_out, out):
    nc = tc.nc
    with ExitStack() as ctx:
        const = ctx.enter_context(tc.tile_pool(name="const", bufs=1))
        rawp = ctx.enter_context(tc.tile_pool(name="rawp", bufs=5))
        srtp = ctx.enter_context(tc.tile_pool(name="srtp", bufs=4))
        grpp = ctx.enter_context(tc.tile_pool(name="grpp", bufs=7))
        keep = ctx.enter_context(tc.tile_pool(name="keep", bufs=1))
        ostp = ctx.enter_context(tc.tile_pool(name="ostp", bufs=5))
        psp = ctx.enter_context(tc.psum_pool(name="psp", bufs=8))
        ctx.enter_context(tc.manual_schedule())

        ident = const.tile([P, P], BF16, name="ident")
        make_identity(nc, ident[:])
        perm = const.tile([P, P], BF16, name="perm")
        nc.vector.tensor_copy(
            out=perm[:].rearrange("p (i c b) -> p i c b", i=2, b=2),
            in_=ident[:].rearrange("p (c i b) -> p i c b", i=2, b=2),
        )

        xc = keep.tile([P, GROUPS * C_IN], U32, name="xc", align_bytes=64)
        xs = keep.tile([P, GROUPS * C_IN], U8, name="xs", align_bytes=64)
        gcs = []
        gss = []
        for c2 in range(2):
            gcs.append(keep.tile([P, GROUPS * 256], U32, name="gc%d" % c2, align_bytes=64))
            gss.append(keep.tile([P, GROUPS * 256], U8, name="gs%d" % c2, align_bytes=64))

        blocks = [(x, k) for k in range(NBX)] + [(grad_out, k) for k in range(NBG)]
        raws = []
        for src, k in blocks:
            raw = rawp.tile([P, PIX], BF16, name="raw")
            nc.sync.dma_start(
                out=raw[:].rearrange("p (b f) -> p b f", b=2),
                in_=src[:, k * BLK : (k + 1) * BLK].rearrange("b c (u h) w -> (c u) b (h w)", u=2),
            )
            raws.append(raw)

        srts = {}
        grps = {}

        def sort_block(s, pieces):
            srt = srtp.tile([P, PIX], BF16, name="srt")
            dst = srt[:].bitcast(F32).rearrange("p (a h r c) -> p a h r c", a=4, h=2, r=16)
            src = raws[s][:].bitcast(F32).rearrange("p (r a c h) -> p a h r c", a=4, h=2, r=16)
            step = 4 // pieces
            for a in range(0, 4, step):
                nc.vector.tensor_copy(out=dst[:, a : a + step], in_=src[:, a : a + step])
            srts[s] = srt

        def grouped(key):
            if key not in grps:
                grps[key] = grpp.tile([P, 4096], BF16, name="grp", align_bytes=64)
            return grps[key]

        def banks(s, pr, halves=(0, 1)):
            is_g = s >= NBX
            words = srts[s][:].rearrange("p (w e) -> p w e", e=2)
            for h in halves:
                tp = psp.tile([P, 512], BF16, name="tp", tag="bank")
                for e in range(2):
                    for rh in range(2):
                        w0 = (pr * 2 + h) * 256 + rh * 128
                        src = words[:, w0 : w0 + 128, e]
                        if is_g:
                            dst = tp[:].rearrange("p (e i r n) -> p e i r n", e=2, i=2, r=2)[:, e, :, rh, :]
                            nc.tensor.transpose(dst, src, perm[:])
                        else:
                            dst = tp[:, (e * 2 + rh) * 128 : (e * 2 + rh + 1) * 128]
                            nc.tensor.transpose(dst, src, ident[:])
                if is_g:
                    kb = (s - NBX) % 4
                    grp = grouped(("g", (s - NBX) // 4, pr))
                    nc.scalar.copy(
                        out=grp[:]
                        .bitcast(F32)
                        .rearrange("p (a m r) -> p a m r", a=8, r=2)[:, h * 4 : h * 4 + 4, kb * 32 : (kb + 1) * 32, :],
                        in_=tp[:].bitcast(F32).rearrange("p (a r c) -> p a c r", a=4, r=2),
                    )
                else:
                    kb = s % 2
                    gl = (pr % 2) * 4 + 2 * h
                    grp = grouped(("x", s // 2, pr // 2))
                    nc.scalar.copy(
                        out=grp[:]
                        .bitcast(F32)
                        .rearrange("p (g c r) -> p g c r", g=8, r=2)[:, gl : gl + 2, kb * 64 : (kb + 1) * 64, :],
                        in_=tp[:].bitcast(F32).rearrange("p (e r c) -> p e c r", e=2, r=2),
                    )

        def quant_x(chunk, grp_no):
            grp = grps[("x", chunk, grp_no // 8)]
            gl = grp_no % 8
            col = grp_no * C_IN + chunk * 128
            nc.vector.quantize_mx(
                out=xc[:, col : col + 128].bitcast(E4X4),
                scales=xs[:, col : col + 128],
                in_=grp[:, gl * 512 : (gl + 1) * 512],
            )

        def quant_g(c2, pr, pairs=(0, 1)):
            for gp in pairs:
                w0 = pr * 1024 + gp * 512
                nc.vector.quantize_mx(
                    out=gcs[c2][:, w0 : w0 + 512].bitcast(E5X4),
                    scales=gss[c2][:, w0 : w0 + 512],
                    in_=grps[("g", c2, pr)][:, gp * 2048 : (gp + 1) * 2048],
                )

        def passes(c2, pr, gp, pattern, fine=False):
            g0 = pr * 4 + gp * 2
            ost = ostp.tile([P, 2, 2, C_IN], F32, name="ost")
            rows = slice(c2 * 256, (c2 + 1) * 256)
            for gl in range(2):
                grp = g0 + gl
                lo = grp * C_IN
                skip = 0
                if lo + 512 > GROUPS * C_IN:
                    skip = lo + 512 - GROUPS * C_IN
                    lo = lo - skip
                for i in range(2):
                    acc = psp.tile([P, 512], F32, name="acc", tag="bank")
                    w0 = (grp * 2 + i) * 128
                    nc.tensor.matmul_mx(
                        out=acc[:],
                        lhsT=gcs[c2][:, w0 : w0 + 128].bitcast(E5X4),
                        lhsT_scale=gss[c2][:, w0 : w0 + 128],
                        rhs=xc[:, lo : lo + 512].bitcast(E4X4),
                        rhs_scale=xs[:, lo : lo + 512],
                        start=True,
                        stop=True,
                    )
                    if pattern[gl * 2 + i] == "V":
                        nc.vector.tensor_copy(out=ost[:, gl, i, :], in_=acc[:, skip : skip + C_IN])
                    else:
                        nc.scalar.copy(out=ost[:, gl, i, :], in_=acc[:, skip : skip + C_IN])
                    if fine and gl == 1:
                        nc.sync.dma_start(
                            out=out[grp, rows, :].rearrange("(m i) c -> i m c", i=2)[i],
                            in_=ost[:, gl, i, :],
                        )
                if fine and gl == 0:
                    nc.sync.dma_start(
                        out=out[grp, rows, :].rearrange("(m i) c -> m (i c)", i=2),
                        in_=ost[:, gl].rearrange("p i c -> p (i c)"),
                    )
            if not fine:
                nc.sync.dma_start(
                    out=out[g0 : g0 + 2, rows, :].rearrange("g (m i) c -> m g (i c)", i=2),
                    in_=ost[:].rearrange("p g i c -> p g (i c)"),
                )

        x_calls = [(chunk, grp_no) for chunk in range(3) for grp_no in range(GROUPS)]
        issued = 0
        sort_block(0, 4)
        for s in range(10):
            if s < 9:
                sort_block(s + 1, 1)
            for pr in range(4):
                banks(s, pr)
            ready = GROUPS * ((min(s, NBX - 1) + 1) // 2)
            upto = min(ready, issued + 6)
            for chunk, grp_no in x_calls[issued:upto]:
                quant_x(chunk, grp_no)
            issued = upto
        assert issued == len(x_calls)
        sort_block(10, 1)
        quant_g(0, 0)
        quant_g(0, 1)
        banks(10, 0)
        quant_g(0, 2)
        passes(0, 0, 0, "SSVS")
        passes(0, 0, 1, "SVSV")
        sort_block(11, 1)
        banks(10, 1)
        passes(0, 1, 0, "SSVS")
        passes(0, 1, 1, "SVSV")
        sort_block(12, 1)
        passes(0, 2, 0, "SSVS")
        passes(0, 2, 1, "SVSV")
        banks(10, 2)
        sort_block(13, 1)
        banks(11, 0)
        banks(11, 1)
        banks(11, 2)
        banks(12, 0)
        quant_g(0, 3)
        banks(12, 1)
        banks(13, 0)
        passes(0, 3, 0, "SVSV")
        quant_g(1, 0)
        passes(0, 3, 1, "SSVS")
        banks(13, 1)
        quant_g(1, 1)
        banks(12, 2)
        banks(13, 2)
        passes(1, 0, 0, "SVSV")
        quant_g(1, 2)
        passes(1, 0, 1, "SSVS")
        passes(1, 1, 0, "SVSV")
        passes(1, 1, 1, "SVSV")
        passes(1, 2, 0, "SVSV")
        passes(1, 2, 1, "SVSV")
        for h in range(2):
            for s in range(10, 14):
                banks(s, 3, (h,))
            quant_g(1, 3, (h,))
        passes(1, 3, 0, "SSVS")
        passes(1, 3, 1, "SVSV", fine=True)
